import numpy as np
import ml_dtypes


def mxq(x, axis, fmt="e4m3"):
    dtype, down = {"e4m3": (ml_dtypes.float8_e4m3fn, 7), "e5m2": (ml_dtypes.float8_e5m2, 14)}[fmt]
    v = np.moveaxis(np.asarray(x, np.float32).astype(ml_dtypes.bfloat16).astype(np.float64), axis, -1)
    blocks = v.reshape(v.shape[:-1] + (-1, 32))
    amax = np.abs(blocks).max(-1, keepdims=True)
    byte = np.maximum(np.where(amax > 0, np.frexp(amax)[1] - 1 + 127, 0) - down, 1)
    scale = np.exp2(byte - 127.0)
    codes = (blocks / scale).astype(np.float32).astype(dtype).astype(np.float64)
    return np.moveaxis((codes * scale).reshape(v.shape), -1, axis)


WIDE = False


def mx_kscale(k):
    if not WIDE:
        return np.ones(k)
    levels = np.array([10, -10, 5, -5, 0])
    if k % 512:
        return np.exp2(np.random.permutation(np.resize(levels, k // 32))).repeat(32)
    a = np.empty((k // 512, 16))
    for p in range(k // 512):
        a[p, :8] = np.random.permutation(np.resize(levels, 8))
        for g in range(8):
            far = levels[np.abs(levels - a[p, g]) >= 10]
            a[p, g + 8] = far[np.random.randint(len(far))]
    return np.exp2(a.ravel()).repeat(32)


BF16 = ml_dtypes.bfloat16


def bf(x):
    return np.asarray(x, np.float32).astype(BF16)


def f64(x):
    return np.asarray(x).astype(np.float64)


B, DIM, D_IN, HID = 2048, 256, 128, 512
D_OUT = DIM - D_IN
LOG_SCALE_CLAMP = 2.0


def _net_draw(c_out):
    k, f = mx_kscale(HID), mx_kscale(HID)
    h = bf(np.maximum(np.random.standard_normal((B, HID)), 0.0) * np.sqrt(2.0) * k)
    w_hid = bf(np.random.standard_normal((HID, HID)) * np.sqrt(2.0 / HID) * f[:, None] / k[None, :])
    b_hid = bf(np.random.standard_normal(HID) * 0.3 * f)
    w_out = bf(np.random.standard_normal((D_OUT, HID)) * c_out / np.sqrt(HID) / f[None, :])
    b_out = bf(np.random.standard_normal(D_OUT) * 0.3)
    return h, w_hid, b_hid, w_out, b_out


def draw0():
    z = bf(np.random.standard_normal((B, DIM)))
    h_s, s_Whid1, s_bhid1, s_Wout, s_bout = _net_draw(1.2)
    h_t, t_Whid1, t_bhid1, t_Wout, t_bout = _net_draw(1.0)
    return {"z": z, "h_s": h_s, "h_t": h_t,
            "s_Whid1": s_Whid1, "s_bhid1": s_bhid1, "s_Wout": s_Wout, "s_bout": s_bout,
            "t_Whid1": t_Whid1, "t_bhid1": t_bhid1, "t_Wout": t_Wout, "t_bout": t_bout}


def _tail(h, w_hid, b_hid, w_out, b_out):
    g = np.maximum((mxq(f64(h), 1, "e4m3") @ mxq(f64(w_hid), 1, "e4m3").T) + f64(b_hid), 0.0)
    return (mxq(g, 1, "e4m3") @ mxq(f64(w_out), 1, "e4m3").T) + f64(b_out)


def core(z, h_s, h_t, s_Whid1, s_bhid1, s_Wout, s_bout, t_Whid1, t_bhid1, t_Wout, t_bout):
    z = f64(z)
    z1 = z[:, :D_IN]
    z2 = z[:, D_IN:]
    log_s = np.clip(_tail(h_s, s_Whid1, s_bhid1, s_Wout, s_bout), -LOG_SCALE_CLAMP, LOG_SCALE_CLAMP)
    t = _tail(h_t, t_Whid1, t_bhid1, t_Wout, t_bout)
    z2_out = z2 * np.exp(log_s) + t
    z_out = np.concatenate([z1, z2_out], axis=1)
    log_det = log_s.sum(axis=-1)
    return (z_out, log_det)


def e4m3fn_bytes(y):
    return np.clip(np.asarray(y, np.float64), -448.0, 448.0).astype(np.float32).astype(ml_dtypes.float8_e4m3fn).view(np.uint8)


def e4m3fn_values(b):
    return np.asarray(b, np.uint8).view(ml_dtypes.float8_e4m3fn).astype(np.float64)


def setup_inputs():
    d = draw0()
    x0 = np.asarray(d['h_t']).astype(np.float64)
    s = (np.max(np.abs(x0), axis=(0,), keepdims=True) / 448.0).astype(np.float32)
    out = {}
    for k, v in d.items():
        if k == 'h_t':
            out['h_t_bytes'] = e4m3fn_bytes(x0 / s.astype(np.float64))
            out['h_t_scale'] = s
        else:
            out[k] = v
    return out


def reference(z, h_s, h_t_bytes, h_t_scale, s_Whid1, s_bhid1, s_Wout, s_bout, t_Whid1, t_bhid1, t_Wout, t_bout):
    return core(z, h_s, e4m3fn_values(h_t_bytes) * h_t_scale.astype(np.float64), s_Whid1, s_bhid1, s_Wout, s_bout, t_Whid1, t_bhid1, t_Wout, t_bout)

from contextlib import ExitStack

import concourse.mybir as mybir
from concourse.masks import make_identity

TOKENS, DIM, HALF, HID = 2048, 256, 128, 512
WEV = "ssss"
RV = []
FLOPS = 2 * 2 * TOKENS * HID * (HID + HALF)

F32 = mybir.dt.float32
BF16 = mybir.dt.bfloat16
U32 = mybir.dt.uint32
U8 = mybir.dt.uint8
FP8 = mybir.dt.float8_e4m3fn
FP8X4 = mybir.dt.float8_e4m3fn_x4
ALU = mybir.AluOpType
ACT = mybir.ActivationFunctionType

P = 128
PACK = 4
TILES = TOKENS // P
GROUP = 4
COLS = GROUP * P
GROUPS = TILES // GROUP
STEPS = 2 * GROUPS
OT = (0, 1, 2)
ORDER = [
    ("SCT",), ("SCE",), ("P", 1, 0), ("P", 1, 2), ("P", 1, 1), ("P", 1, 3), ("WT", 0, 0), ("WE", 0, 0),
    ("WT", 0, 1), ("WE", 0, 1), ("WQ", 0), ("T", 0, 0), ("E", 0, 0), ("T", 0, 1), ("E", 0, 1), ("QH", 0),
    ("T", 1, 0), ("E", 1, 0), ("T", 1, 1), ("E", 1, 1), ("QH", 1), ("P", 3, 0), ("M", 0, 0), ("R", 0, 0),
    ("WT", 1, 0), ("WE", 1, 0), ("WT", 1, 1), ("WE", 1, 1), ("WQ", 1), ("M", 0, 1), ("R", 0, 1), ("P", 3, 2),
    ("M", 0, 2), ("R", 0, 2), ("M", 0, 3), ("R", 0, 3), ("I", 0), ("P", 3, 1), ("P", 3, 3), ("QG", 0),
    ("WO", 1), ("WOE", 1), ("WOQ", 1), ("M", 1, 0), ("R", 1, 0), ("WO", 0), ("WOE", 0), ("WOQ", 0),
    ("T", 2, 0), ("E", 2, 0), ("M", 1, 1), ("R", 1, 1), ("T", 2, 1), ("E", 2, 1), ("QH", 2), ("M", 1, 2),
    ("R", 1, 2), ("M", 1, 3), ("R", 1, 3), ("I", 1), ("QG", 1), ("T", 3, 0), ("E", 3, 0), ("S2", 0),
    ("Y", 0), ("CL", 0), ("T", 3, 1), ("E", 3, 1), ("QH", 3), ("P", 5, 0), ("M", 2, 0), ("R", 2, 0),
    ("M", 2, 1), ("R", 2, 1), ("P", 5, 2), ("M", 2, 2), ("R", 2, 2), ("M", 2, 3), ("R", 2, 3), ("I", 2),
    ("P", 5, 1), ("P", 5, 3), ("QG", 2), ("LT", 0), ("X", 0), ("MU", 0), ("M", 3, 0), ("R", 3, 0),
    ("T", 4, 0), ("E", 4, 0), ("M", 3, 1), ("R", 3, 1), ("T", 4, 1), ("E", 4, 1), ("QH", 4), ("M", 3, 2),
    ("R", 3, 2), ("M", 3, 3), ("R", 3, 3), ("I", 3), ("QG", 3), ("S2", 1), ("OY", 0), ("T", 5, 0),
    ("E", 5, 0), ("S2", 2), ("Y", 1), ("CL", 1), ("T", 5, 1), ("E", 5, 1), ("QH", 5), ("OB", 0),
    ("AD", 0), ("P", 7, 0), ("M", 4, 0), ("R", 4, 0), ("M", 4, 1), ("R", 4, 1), ("P", 7, 2), ("M", 4, 2),
    ("R", 4, 2), ("M", 4, 3), ("R", 4, 3), ("I", 4), ("P", 7, 1), ("P", 7, 3), ("QG", 4), ("LD", 0),
    ("LE", 0), ("LT", 1), ("X", 1), ("MU", 1), ("M", 5, 0), ("R", 5, 0), ("T", 6, 0), ("E", 6, 0),
    ("M", 5, 1), ("R", 5, 1), ("T", 6, 1), ("E", 6, 1), ("QH", 6), ("M", 5, 2), ("R", 5, 2), ("M", 5, 3),
    ("R", 5, 3), ("I", 5), ("QG", 5), ("S2", 3), ("OY", 1), ("T", 7, 0), ("E", 7, 0), ("S2", 4),
    ("Y", 2), ("CL", 2), ("T", 7, 1), ("E", 7, 1), ("QH", 7), ("OB", 1), ("AD", 1), ("M", 6, 0),
    ("R", 6, 0), ("M", 6, 1), ("R", 6, 1), ("M", 6, 2), ("R", 6, 2), ("M", 6, 3), ("R", 6, 3), ("I", 6),
    ("QG", 6), ("LD", 1), ("LE", 1), ("LT", 2), ("X", 2), ("MU", 2), ("M", 7, 0), ("R", 7, 0),
    ("M", 7, 1), ("R", 7, 1), ("M", 7, 2), ("R", 7, 2), ("M", 7, 3), ("R", 7, 3), ("I", 7, 0), ("QG", 7, 0),
    ("S2", 5), ("OY", 2), ("S2", 6), ("Y", 3), ("CL", 3), ("OB", 2), ("AD", 2), ("I", 7, 1),
    ("QG", 7, 1), ("LD", 2), ("LE", 2), ("LT", 3), ("X", 3), ("MU", 3), ("BT", 3), ("S2", 7, 0),
    ("AD", 3, 0), ("S2", 7, 1), ("AD", 3, 1), ("LD", 3), ("LE", 3),
]


def tile_affinecouplinglayer_pa_kernel(
    tc, z, h_s, h_t_bytes, h_t_scale, s_Whid1, s_bhid1, s_Wout, s_bout,
    t_Whid1, t_bhid1, t_Wout, t_bout, out_0, out_1,
):
    nc = tc.nc
    with ExitStack() as ctx:
        keep = ctx.enter_context(tc.tile_pool(name="keep", bufs=1))
        work = ctx.enter_context(tc.tile_pool(name="work", bufs=3))
        ps_x = ctx.enter_context(tc.psum_pool(name="ps_x", bufs=4))
        ps_t = ctx.enter_context(tc.psum_pool(name="ps_t", bufs=2))
        ps_a = ctx.enter_context(tc.psum_pool(name="ps_a", bufs=1))
        ps_b = ctx.enter_context(tc.psum_pool(name="ps_b", bufs=1))

        ident = keep.tile([P, P], F32, name="ident")
        make_identity(nc, ident[:])
        ones = keep.tile([P, 1], F32, name="ones")
        nc.gpsimd.memset(ones[:], 1.0)
        warm = keep.tile([P, 1], F32, name="warm")

        hs_sb = keep.tile([P, TILES, HID], BF16, name="hs_sb")
        ht_bytes = keep.tile([P, TILES, HID], U8, name="ht_bytes", align_bytes=64)
        z_sb = keep.tile([P, TILES, DIM], BF16, name="z_sb")
        w_raw = [keep.tile([P, PACK, HID], BF16, name="w_raw_s"), keep.tile([P, PACK, HID], BF16, name="w_raw_t")]
        wo_raw = [keep.tile([P, HID], BF16, name="wo_raw_s"), keep.tile([P, HID], BF16, name="wo_raw_t")]
        b_hid = [keep.tile([P, PACK], BF16, name="b_hid_s"), keep.tile([P, PACK], BF16, name="b_hid_t")]
        b_s = keep.tile([P, 1], BF16, name="b_s")
        b_t = keep.tile([P, HALF], BF16, name="b_t")
        b_tc = keep.tile([P, 1], BF16, name="b_tc")
        scale_col = keep.tile([P, PACK], F32, name="scale_col")
        scale_row = keep.tile([P, HID], F32, name="scale_row", align_bytes=64)

        hs_v = h_s.rearrange("(p i) k -> p i k", p=P)
        ht_v = h_t_bytes.rearrange("(p i) k -> p i k", p=P)
        z_v = z.rearrange("(p i) d -> p i d", p=P)
        out_v = out_0.rearrange("(p i) d -> p i d", p=P)
        w_v = [s_Whid1.rearrange("(m t) k -> m t k", t=PACK), t_Whid1.rearrange("(m t) k -> m t k", t=PACK)]

        nc.scalar.dma_start(out=scale_col[:], in_=h_t_scale.rearrange("o (p c) -> p (o c)", c=PACK))
        nc.scalar.dma_start(out=b_hid[0][:], in_=s_bhid1.rearrange("(p t) -> p t", t=PACK))
        nc.scalar.dma_start(out=b_s[:], in_=s_bout.rearrange("(p o) -> p o", o=1))
        nc.scalar.dma_start(out=b_hid[1][:], in_=t_bhid1.rearrange("(p t) -> p t", t=PACK))
        nc.scalar.dma_start(out=b_tc[:], in_=t_bout.rearrange("(p o) -> p o", o=1))

        def load_tiles(dst, src, a, b):
            nc.sync.dma_start(out=dst[:, a:b, :], in_=src[:, a:b, :])

        load_tiles(ht_bytes, ht_v, 0, 4)
        load_tiles(w_raw[0], w_v[0], 0, 2)
        load_tiles(w_raw[0], w_v[0], 2, 4)
        load_tiles(hs_sb, hs_v, 0, 2)
        load_tiles(hs_sb, hs_v, 2, 4)
        nc.sync.dma_start(out=wo_raw[0][:], in_=s_Wout)
        load_tiles(w_raw[1], w_v[1], 0, 2)
        load_tiles(w_raw[1], w_v[1], 2, 4)
        load_tiles(ht_bytes, ht_v, 4, 8)
        load_tiles(hs_sb, hs_v, 4, 6)
        load_tiles(hs_sb, hs_v, 6, 8)
        nc.sync.dma_start(out=wo_raw[1][:], in_=t_Wout)
        load_tiles(z_sb, z_v, 0, 4)
        load_tiles(ht_bytes, ht_v, 8, 12)
        load_tiles(hs_sb, hs_v, 8, 10)
        load_tiles(hs_sb, hs_v, 10, 12)
        load_tiles(z_sb, z_v, 4, 8)
        load_tiles(ht_bytes, ht_v, 12, 16)
        load_tiles(hs_sb, hs_v, 12, 14)
        load_tiles(hs_sb, hs_v, 14, 16)
        nc.sync.dma_start(out=b_t[:], in_=t_bout.partition_broadcast(P))
        load_tiles(z_sb, z_v, 8, 12)
        load_tiles(z_sb, z_v, 12, 16)

        ctx.enter_context(tc.manual_schedule())

        nc.scalar.activation(out=warm[:], in_=ones[:], func=ACT.Exp)

        w_grp = [keep.tile([P, HID, PACK], BF16, name="w_grp_s", align_bytes=64), keep.tile([P, HID, PACK], BF16, name="w_grp_t", align_bytes=64)]
        w_codes = [keep.tile([P, HID], U32, name="w_codes_s", align_bytes=64), keep.tile([P, HID], U32, name="w_codes_t", align_bytes=64)]
        w_scales = [keep.tile([P, HID], U8, name="w_scales_s", align_bytes=64), keep.tile([P, HID], U8, name="w_scales_t", align_bytes=64)]
        wo_grp = [keep.tile([P, HALF, PACK], BF16, name="wo_grp_s", align_bytes=64), keep.tile([P, HALF, PACK], BF16, name="wo_grp_t", align_bytes=64)]
        wo_codes = [keep.tile([P, HALF], U32, name="wo_codes_s", align_bytes=64), keep.tile([P, HALF], U32, name="wo_codes_t", align_bytes=64)]
        wo_scales = [keep.tile([P, HALF], U8, name="wo_scales_s", align_bytes=64), keep.tile([P, HALF], U8, name="wo_scales_t", align_bytes=64)]
        ld_sb = keep.tile([P, TILES], F32, name="ld_sb")

        def flat(t):
            return t[:].rearrange("p n j -> p (n j)")

        def copy(engine, out, in_):
            if engine == "v":
                nc.vector.tensor_copy(out=out, in_=in_)
            else:
                nc.scalar.copy(out=out, in_=in_)

        def turn(bank, rows):
            for i, r in enumerate(rows):
                words = r.bitcast(F32)
                for u in (0, 1):
                    nc.tensor.transpose(bank[:, i, u, :], words[:, u : HID // 2 : 2], ident[:])

        def empty(engine, grp, bank, first, count):
            words = flat(grp).bitcast(F32)
            dst = words[:, first * 256 : (first + count) * 256].rearrange("p (i n u) -> p i n u", i=count, u=2)
            copy(engine, dst, bank[:, 0:count, :, :].rearrange("p i u n -> p i n u"))

        def quantize(codes, scales, grp):
            nc.vector.quantize_mx(out=codes[:].bitcast(FP8X4), scales=scales[:], in_=flat(grp))

        def x_bank():
            b = ps_x.tile([P, COLS], F32, name="x_bank")
            return b

        def t_bank():
            b = ps_t.tile([P, COLS], F32, name="t_bank")
            return b

        def as4(b):
            return b[:].rearrange("p (i u n) -> p i u n", i=2, u=2)

        def w_turn(net, get):
            banks = []
            for half in range(2):
                b = as4(get())
                turn(b, [w_raw[net][:, 2 * half + i, :] for i in range(2)])
                banks.append(b)
            return banks

        def wo_turn(net, get):
            b = as4(get())
            turn(b[:, 0:1], [wo_raw[net][:]])
            return b

        st = {}

        def get(kind, j, make):
            if (kind, j) not in st:
                st[kind, j] = make()
            return st[kind, j]

        def new(shape, dt, name):
            t = work.tile(shape, dt, name=name, align_bytes=64)
            return t

        def copy_words(engine, grp, bank, first, count):
            empty(engine, grp, bank, first, count)

        def do_SCT():
            sb = x_bank()
            for c in range(PACK):
                nc.tensor.transpose(sb[:, P * c : P * (c + 1)], scale_col[:, c : c + 1].to_broadcast([P, P]), ident[:])
            st["sc"] = sb

        def do_SCE():
            nc.scalar.copy(out=scale_row[:].rearrange("p (k c) -> p k c", c=PACK), in_=st["sc"][:].rearrange("p (c k) -> p k c", c=PACK))

        def do_WT(net, h):
            b = as4(x_bank() if net == 0 else t_bank())
            turn(b, [w_raw[net][:, 2 * h + i, :] for i in range(2)])
            st["wb", net, h] = b

        def do_WE(net, h):
            empty(WEV[2 * net + h], w_grp[net], st["wb", net, h], 2 * h, 2)

        def do_WQ(net):
            quantize(w_codes[net], w_scales[net], w_grp[net])

        def do_WO(net):
            b = as4(x_bank() if net == 0 else t_bank())
            turn(b[:, 0:1], [wo_raw[net][:]])
            st["wob", net] = b

        def do_WOE(net):
            empty("s", wo_grp[net], st["wob", net], 0, 1)

        def do_WOQ(net):
            quantize(wo_codes[net], wo_scales[net], wo_grp[net])

        def do_P(j, i):
            t = get("ht", j, lambda: new([P, GROUP, HID], BF16, "ht_bf"))
            nc.vector.tensor_tensor(
                out=t[:, i, :], in0=ht_bytes[:, GROUP * (j // 2) + i, :].bitcast(FP8), in1=scale_row[:], op=ALU.mult)

        def do_T(j, h):
            b = as4(t_bank())
            if j % 2 == 0:
                rows = [hs_sb[:, GROUP * (j // 2) + 2 * h + i, :] for i in range(2)]
            else:
                rows = [st["ht", j][:, 2 * h + i, :] for i in range(2)]
            turn(b, rows)
            st["tb", j, h] = b

        def do_E(j, h):
            grp = get("hg", j, lambda: new([P, COLS, PACK], BF16, "h_grp"))
            empty("s", grp, st["tb", j, h], 2 * h, 2)

        def do_QH(j):
            codes = new([P, COLS], U32, "h_codes")
            scales = new([P, COLS], U8, "h_scales")
            quantize(codes, scales, st["hg", j])
            st["hc", j] = (codes, scales)

        def do_M(j, t):
            net = j % 2
            codes, scales = st["hc", j]
            b = x_bank()
            nc.tensor.matmul_mx(
                out=b[:],
                lhsT=w_codes[net][:, P * t : P * (t + 1)].bitcast(FP8X4),
                lhsT_scale=w_scales[net][:, P * t : P * (t + 1)],
                rhs=codes[:].bitcast(FP8X4), rhs_scale=scales[:],
                start=True, stop=True)
            st["x", j, t] = b

        def do_R(j, t):
            gp = get("gp", j, lambda: new([P, PACK, COLS], BF16, "g_planes"))
            if (j, t) in RV:
                nc.vector.tensor_scalar(out=gp[:, t, :], in0=st["x", j, t][:], scalar1=b_hid[j % 2][:, t : t + 1], scalar2=0.0, op0=ALU.add, op1=ALU.max)
            else:
                nc.scalar.activation(out=gp[:, t, :], in_=st["x", j, t][:], func=ACT.Relu, bias=b_hid[j % 2][:, t : t + 1])

        def inter(j, engine="v", a=0, b=COLS):
            if ("gg", j) not in st:
                t = work.tile([P, COLS, PACK], BF16, name="g_grp", align_bytes=64)
                st["gg", j] = t
            copy(engine,
                 st["gg", j][:, a:b, :].rearrange("p (c i) t -> p c t i", i=4),
                 st["gp", j][:, :, a:b].rearrange("p t (c i) -> p c t i", i=4))

        def qg(j, a=0, b=COLS):
            if ("gc", j) not in st:
                codes = work.tile([P, COLS], U32, name="g_codes", align_bytes=64)
                scales = work.tile([P, COLS], U8, name="g_scales", align_bytes=64)
                st["gc", j] = (codes, scales)
            codes, scales = st["gc", j]
            nc.vector.quantize_mx(
                out=codes[:, a:b].bitcast(FP8X4), scales=scales[:, a:b],
                in_=st["gg", j][:, a:b, :].rearrange("p n j -> p (n j)"))

        def st2_rows(net, codes, scales):
            b = (ps_a if net == 0 else ps_b).tile([P, COLS], F32, name="a_bank" if net == 0 else "b_bank")
            nc.tensor.matmul_mx(
                out=b[:], lhsT=wo_codes[net][:].bitcast(FP8X4), lhsT_scale=wo_scales[net][:],
                rhs=codes[:].bitcast(FP8X4), rhs_scale=scales[:], start=True, stop=True)
            return b

        def st2(j, a=0, b=GROUP):
            net = j % 2
            codes, scales = st["gc", j]
            if net == 0 or (j // 2) in OT:
                st["o", j] = st2_rows(net, codes, scales)
                return
            if ("o", j) not in st:
                t = ps_b.tile([P, COLS], F32, name="b_bank")
                st["o", j] = t
            for i in range(a, b):
                nc.tensor.matmul_mx(
                    out=st["o", j][:, P * i : P * (i + 1)],
                    lhsT=codes[:, P * i : P * (i + 1)].bitcast(FP8X4), lhsT_scale=scales[:, P * i : P * (i + 1)],
                    rhs=wo_codes[1][:].bitcast(FP8X4), rhs_scale=wo_scales[1][:], start=True, stop=True)

        def s_bias(g):
            y = work.tile([P, COLS], F32, name="y_t")
            nc.scalar.activation(out=y[:], in_=st["o", 2 * g][:], func=ACT.Identity, bias=b_s[:])
            st["y", g] = y

        def s_clip(g):
            ls = work.tile([P, COLS], F32, name="ls_t")
            nc.vector.tensor_scalar(out=ls[:], in0=st["y", g][:], scalar1=2.0, scalar2=-2.0, op0=ALU.min, op1=ALU.max)
            st["ls", g] = ls

        def s_turn(g):
            b = ps_a.tile([P, COLS], F32, name="a_bank")
            for i in range(GROUP):
                nc.tensor.transpose(b[:, P * i : P * (i + 1)], st["ls", g][:, P * i : P * (i + 1)], ident[:])
            st["lsT", g] = b

        def s_sum(g):
            ld = t_bank()
            for i in range(GROUP):
                nc.tensor.matmul(ld[:, i : i + 1], lhsT=st["ls", g][:, P * i : P * (i + 1)], rhs=ones[:], start=True, stop=True)
            st["ld", g] = ld

        def s_exp(g):
            e = work.tile([P, COLS], F32, name="e_t")
            nc.scalar.activation(out=e[:], in_=st["lsT", g][:], func=ACT.Exp)
            st["e", g] = e

        def s_sum_out(g):
            nc.scalar.copy(out=ld_sb[:, GROUP * g : GROUP * (g + 1)], in_=st["ld", g][:, 0:GROUP])

        def t_scale(g):
            w = work.tile([P, GROUP, HALF], F32, name="w_t")
            nc.vector.tensor_tensor(out=w[:], in0=z_sb[:, GROUP * g : GROUP * (g + 1), HALF:DIM],
                                    in1=st["e", g][:].rearrange("p (i d) -> p i d", i=GROUP), op=ALU.mult)
            st["w", g] = w

        def t_bias(g):
            w = work.tile([P, GROUP, HALF], F32, name="v_t")
            nc.vector.tensor_tensor(
                out=w[:], in0=st["w", g][:], in1=b_t[:].unsqueeze(1).to_broadcast([P, GROUP, HALF]), op=ALU.add)
            st["w", g] = w

        def o_bias(g):
            y = work.tile([P, COLS], F32, name="oy_t")
            nc.scalar.activation(out=y[:], in_=st["o", 2 * g + 1][:], func=ACT.Identity, bias=b_tc[:])
            st["oy", g] = y

        def o_turn(g):
            b = ps_b.tile([P, COLS], F32, name="b_bank")
            for i in range(GROUP):
                nc.tensor.transpose(b[:, P * i : P * (i + 1)], st["oy", g][:, P * i : P * (i + 1)], ident[:])
            st["o", 2 * g + 1] = b

        def z_copy(g):
            o = work.tile([P, GROUP, DIM], F32, name="z_out")
            nc.gpsimd.tensor_scalar(out=o[:, :, 0:HALF], in0=z_sb[:, GROUP * g : GROUP * (g + 1), 0:HALF],
                                    scalar1=1.0, scalar2=0.0, op0=ALU.mult, op1=ALU.add)
            st["zo", g] = o

        def t_add(g, a=0, b=GROUP):
            o = st["zo", g]
            nc.vector.tensor_tensor(
                out=o[:, a:b, HALF:DIM],
                in0=st["o", 2 * g + 1][:].rearrange("p (i d) -> p i d", i=GROUP)[:, a:b, :], in1=st["w", g][:, a:b, :], op=ALU.add)
            nc.sync.dma_start(out=out_v[:, GROUP * g + a : GROUP * g + b, :], in_=o[:, a:b, :])
        def half(f, j, h):
            f(j, h * COLS // 2, (h + 1) * COLS // 2)

        def do_I(j, h=None):
            if h is None:
                inter(j)
            else:
                inter(j, "vs"[h], h * COLS // 2, (h + 1) * COLS // 2)

        def do_QG(j, h=None):
            if h is None:
                qg(j)
            else:
                qg(j, h * COLS // 2, (h + 1) * COLS // 2)

        def do_S2(j, h=None):
            if h is None:
                st2(j)
            else:
                st2(j, 2 * h, 2 * h + 2)

        def do_MU(g):
            t_scale(g)
            z_copy(g)

        def do_AD(g, h=None):
            if h is None:
                t_add(g)
            else:
                t_add(g, 2 * h, 2 * h + 2)

        do = dict(SCT=do_SCT, SCE=do_SCE, WT=do_WT, WE=do_WE, WQ=do_WQ, WO=do_WO, WOE=do_WOE, WOQ=do_WOQ, P=do_P, T=do_T, E=do_E,
                  QH=do_QH, M=do_M, R=do_R, I=do_I, QG=do_QG, S2=do_S2, Y=s_bias, CL=s_clip, LT=s_turn, LD=s_sum, LE=s_sum_out,
                  X=s_exp, MU=do_MU, BT=t_bias, OY=o_bias, OB=o_turn, AD=do_AD)
        for step in ORDER:
            do[step[0]](*step[1:])
        nc.scalar.dma_start(out=out_1.rearrange("(p i) -> p i", p=P), in_=ld_sb[:])
